import numpy as np
import ml_dtypes


def mxq(x, axis, fmt="e4m3"):
    dtype, down = {"e4m3": (ml_dtypes.float8_e4m3fn, 7), "e5m2": (ml_dtypes.float8_e5m2, 14)}[fmt]
    v = np.moveaxis(np.asarray(x, np.float32).astype(ml_dtypes.bfloat16).astype(np.float64), axis, -1)
    blocks = v.reshape(v.shape[:-1] + (-1, 32))
    amax = np.abs(blocks).max(-1, keepdims=True)
    byte = np.maximum(np.where(amax > 0, np.frexp(amax)[1] - 1 + 127, 0) - down, 1)
    scale = np.exp2(byte - 127.0)
    codes = (blocks / scale).astype(np.float32).astype(dtype).astype(np.float64)
    return np.moveaxis((codes * scale).reshape(v.shape), -1, axis)


WIDE = False


def mx_kscale(k):
    if not WIDE:
        return np.ones(k)
    levels = np.array([10, -10, 5, -5, 0])
    if k % 512:
        return np.exp2(np.random.permutation(np.resize(levels, k // 32))).repeat(32)
    a = np.empty((k // 512, 16))
    for p in range(k // 512):
        a[p, :8] = np.random.permutation(np.resize(levels, 8))
        for g in range(8):
            far = levels[np.abs(levels - a[p, g]) >= 10]
            a[p, g + 8] = far[np.random.randint(len(far))]
    return np.exp2(a.ravel()).repeat(32)


BF16 = ml_dtypes.bfloat16


def bf(x):
    return np.asarray(x, np.float32).astype(BF16)


def f64(x):
    return np.asarray(x).astype(np.float64)


B, C, V, K, OUT = 4, 128, 2048, 4, 128


def setup_inputs():
    s = mx_kscale(V)
    g = np.random.standard_normal((V, V))
    lap = (g + g.T) * (0.45 / np.sqrt(V))
    return {"input": bf(np.random.standard_normal((B, C, V)) * s),
            "laplacian": bf(lap * s[:, None] / s[None, :])}


def reference(input, laplacian):
    x0 = f64(input).transpose(2, 1, 0).reshape(V, C * B)
    lq = mxq(f64(laplacian), 1, "e4m3")
    x1 = lq @ mxq(x0, 0, "e4m3")
    x2 = 2.0 * (lq @ mxq(x1, 0, "e4m3")) - x0
    return x1, x2

@@ -1,0 +1,200 @@
+from contextlib import ExitStack
+
+import concourse.mybir as mybir
+from concourse.masks import make_identity
+
+F32 = mybir.dt.float32
+BF16 = mybir.dt.bfloat16
+U32 = mybir.dt.uint32
+U8 = mybir.dt.uint8
+FP8X4 = mybir.dt.float8_e4m3fn_x4
+
+P = 128
+PACK = 4
+V = 2048
+BATCH = 4
+COLS = 512
+PASSES = V // (P * PACK)
+ROW_TILES = V // P
+PAIRS = ROW_TILES // 2
+ROW_WORDS = V // 2
+TILE_CODES = PASSES * P
+PSUM_BANKS = 8
+
+FLOPS = 2 * 2 * V * V * COLS
+
+
+def pass_rows(matrix, g):
+    return matrix[PACK * P * g : PACK * P * (g + 1), :].rearrange("(p t) c -> p t c", t=PACK)
+
+
+def tile_graph_conv_pa_kernel(tc, signal, laplacian, x1_out, x2_out):
+    nc = tc.nc
+    with ExitStack() as ctx:
+        keep = ctx.enter_context(tc.tile_pool(name="keep", bufs=1))
+        lap_rows = ctx.enter_context(tc.tile_pool(name="lap_rows", bufs=PAIRS))
+        lap_stage = ctx.enter_context(tc.tile_pool(name="lap_stage", bufs=2))
+        x1_stage = ctx.enter_context(tc.tile_pool(name="x1_stage", bufs=2))
+        x2_stage = ctx.enter_context(tc.tile_pool(name="x2_stage", bufs=3))
+        psum = ctx.enter_context(tc.psum_pool(name="psum", bufs=PSUM_BANKS))
+        ctx.enter_context(tc.manual_schedule())
+
+        identity = keep.tile([P, P], F32)
+        signal_rows = keep.tile([P, BATCH * V], BF16)
+        x0_grouped = keep.tile([P, PASSES * COLS * PACK], BF16, align_bytes=64)
+        x0_codes = keep.tile([P, PASSES * COLS], U32, align_bytes=64)
+        x0_scales = keep.tile([P, PASSES * COLS], U8, align_bytes=64)
+        x1_codes = keep.tile([P, PASSES * COLS], U32, align_bytes=64)
+        x1_scales = keep.tile([P, PASSES * COLS], U8, align_bytes=64)
+        lap_codes = keep.tile([P, ROW_TILES * TILE_CODES], U32, align_bytes=64)
+        lap_scales = keep.tile([P, ROW_TILES * TILE_CODES], U8, align_bytes=64)
+
+        for b in range(BATCH):
+            nc.sync.dma_start(out=signal_rows[:, b * V : (b + 1) * V], in_=signal[b, :, :])
+        lap_pairs = []
+        for r in range(PAIRS):
+            pair_rows = lap_rows.tile([P, 2 * V], BF16, name="pair_rows")
+            g_rows, u_rows = divmod(r, 2)
+            nc.sync.dma_start(
+                out=pair_rows[:].rearrange("p (e k) -> p e k", e=2),
+                in_=pass_rows(laplacian, g_rows)[:, 2 * u_rows : 2 * u_rows + 2, :],
+            )
+            lap_pairs.append(pair_rows)
+
+        make_identity(nc, identity[:])
+
+        def new_bank():
+            return psum.tile([P, COLS], F32, name="bank")
+
+        def transpose_words(bank, j, words, first_word):
+            nc.tensor.transpose(
+                bank[:, j * P : (j + 1) * P],
+                words[:, first_word : first_word + 2 * P - 1 : 2],
+                identity[:],
+            )
+
+        signal_words = signal_rows[:].bitcast(F32)
+        x0_words = x0_grouped[:].bitcast(F32).rearrange(
+            "p (g c b u) -> p g c b u", g=PASSES, c=P, b=BATCH, u=2
+        )
+        for h in range(2):
+            banks = []
+            for g in range(PASSES):
+                banks.append(new_bank())
+            for b in (2 * h, 2 * h + 1):
+                for g in range(PASSES):
+                    for u in range(2):
+                        transpose_words(
+                            banks[g], 2 * (b % 2) + u, signal_words, b * ROW_WORDS + 2 * g * P + u
+                        )
+            for g in range(PASSES):
+                copy = nc.scalar.copy if g % 2 == 0 else nc.vector.tensor_copy
+                copy(
+                    out=x0_words[:, g, :, 2 * h : 2 * h + 2, :],
+                    in_=banks[g][:].rearrange("p (b u c) -> p c b u", b=2, u=2),
+                )
+        for g in range(PASSES):
+            nc.vector.quantize_mx(
+                out=x0_codes[:, g * COLS : (g + 1) * COLS].bitcast(FP8X4),
+                scales=x0_scales[:, g * COLS : (g + 1) * COLS],
+                in_=x0_grouped[:, g * COLS * PACK : (g + 1) * COLS * PACK],
+            )
+
+        def quantise_pair(r):
+            words = lap_pairs[r][:].bitcast(F32)
+            grouped = lap_stage.tile([P, 2 * TILE_CODES * PACK], BF16, name="grouped", align_bytes=64)
+            grouped_words = grouped[:].bitcast(F32).rearrange(
+                "p (n g i u) -> p n g i u", n=4, g=2, i=P, u=2
+            )
+            banks = []
+            for n in range(4):
+                bank = new_bank()
+                for j in range(4):
+                    transpose_words(bank, j, words, (4 * n + 2 * (j // 2)) * P + j % 2)
+                banks.append(bank)
+            for n in range(4):
+                nc.scalar.copy(
+                    out=grouped_words[:, n],
+                    in_=banks[n][:].rearrange("p (g u i) -> p g i u", g=2, u=2),
+                )
+            for e in range(2):
+                m = 2 * r + e
+                nc.vector.quantize_mx(
+                    out=lap_codes[:, m * TILE_CODES : (m + 1) * TILE_CODES].bitcast(FP8X4),
+                    scales=lap_scales[:, m * TILE_CODES : (m + 1) * TILE_CODES],
+                    in_=grouped[:, e * TILE_CODES * PACK : (e + 1) * TILE_CODES * PACK],
+                )
+
+        def multiply(acc, m, g, x_codes, x_scales):
+            rows = slice((m * PASSES + g) * P, (m * PASSES + g + 1) * P)
+            cols = slice(g * COLS, (g + 1) * COLS)
+            nc.tensor.matmul_mx(
+                out=acc[:],
+                lhsT=lap_codes[:, rows].bitcast(FP8X4),
+                lhsT_scale=lap_scales[:, rows],
+                rhs=x_codes[:, cols].bitcast(FP8X4),
+                rhs_scale=x_scales[:, cols],
+                start=(g == 0),
+                stop=(g == PASSES - 1),
+            )
+
+        def pair_of_rows(out, r):
+            g_rows, u_rows = divmod(r, 2)
+            return pass_rows(out, g_rows)[:, 2 * u_rows : 2 * u_rows + 2, :]
+
+        quantise_pair(0)
+        x1_rows = None
+        for r in range(PAIRS):
+            if r + 1 < PAIRS:
+                quantise_pair(r + 1)
+            g_out, u_out = divmod(r, 2)
+            if u_out == 0:
+                x1_rows = x1_stage.tile([P, PACK, COLS], F32, name="x1_rows")
+            for e in range(2):
+                acc = new_bank()
+                for g in range(PASSES):
+                    multiply(acc, 2 * r + e, g, x0_codes, x0_scales)
+                nc.scalar.copy(out=x1_rows[:, 2 * u_out + e, :], in_=acc[:])
+            nc.sync.dma_start(out=pair_of_rows(x1_out, r), in_=x1_rows[:, 2 * u_out : 2 * u_out + 2, :])
+            if u_out == 1:
+                x1_grouped = x1_stage.tile([P, COLS, PACK], BF16, name="x1_grouped", align_bytes=64)
+                nc.vector.tensor_copy(out=x1_grouped[:], in_=x1_rows[:].rearrange("p t c -> p c t"))
+                nc.vector.quantize_mx(
+                    out=x1_codes[:, g_out * COLS : (g_out + 1) * COLS].bitcast(FP8X4),
+                    scales=x1_scales[:, g_out * COLS : (g_out + 1) * COLS],
+                    in_=x1_grouped[:].rearrange("p c t -> p (c t)"),
+                )
+
+        x0_values = x0_grouped[:].rearrange("p (g c t) -> p g c t", g=PASSES, c=COLS, t=PACK)
+        x2_rows_of_pair = {}
+
+        def finish_x2(acc, m):
+            r, e = divmod(m, 2)
+            g_out, u_out = divmod(r, 2)
+            if e == 0:
+                x2_rows_of_pair[r] = x2_stage.tile([P, 2, COLS], F32, name="x2_rows")
+            x2_rows = x2_rows_of_pair[r]
+            nc.vector.scalar_tensor_tensor(
+                out=x2_rows[:, e, :],
+                in0=acc[:],
+                scalar=2.0,
+                in1=x0_values[:, g_out, :, 2 * u_out + e],
+                op0=mybir.AluOpType.mult,
+                op1=mybir.AluOpType.subtract,
+            )
+            if e == 1:
+                nc.sync.dma_start(out=pair_of_rows(x2_out, r), in_=x2_rows[:])
+
+        accs = []
+        for m in range(PSUM_BANKS):
+            accs.append(new_bank())
+        for g in range(PASSES):
+            for m in range(PSUM_BANKS):
+                multiply(accs[m], m, g, x1_codes, x1_scales)
+                if g == PASSES - 1:
+                    finish_x2(accs[m], m)
+        for m in range(PSUM_BANKS, ROW_TILES):
+            acc = new_bank()
+            for g in range(PASSES):
+                multiply(acc, m, g, x1_codes, x1_scales)
+            finish_x2(acc, m)

@@ -33,6 +33,7 @@ def tile_graph_conv_pa_kernel(tc, signal, laplacian, x1_out, x2_out):
     with ExitStack() as ctx:
         keep = ctx.enter_context(tc.tile_pool(name="keep", bufs=1))
         lap_rows = ctx.enter_context(tc.tile_pool(name="lap_rows", bufs=PAIRS))
+        lap_sorted = ctx.enter_context(tc.tile_pool(name="lap_sorted", bufs=2))
         lap_stage = ctx.enter_context(tc.tile_pool(name="lap_stage", bufs=2))
         x1_stage = ctx.enter_context(tc.tile_pool(name="x1_stage", bufs=2))
         x2_stage = ctx.enter_context(tc.tile_pool(name="x2_stage", bufs=3))
@@ -66,10 +67,10 @@ def tile_graph_conv_pa_kernel(tc, signal, laplacian, x1_out, x2_out):
         def new_bank():
             return psum.tile([P, COLS], F32, name="bank")
 
-        def transpose_words(bank, j, words, first_word):
+        def transpose_words(bank, j, words, first_word, step):
             nc.tensor.transpose(
                 bank[:, j * P : (j + 1) * P],
-                words[:, first_word : first_word + 2 * P - 1 : 2],
+                words[:, first_word : first_word + step * (P - 1) + 1 : step],
                 identity[:],
             )
 
@@ -85,7 +86,7 @@ def tile_graph_conv_pa_kernel(tc, signal, laplacian, x1_out, x2_out):
                 for g in range(PASSES):
                     for u in range(2):
                         transpose_words(
-                            banks[g], 2 * (b % 2) + u, signal_words, b * ROW_WORDS + 2 * g * P + u
+                            banks[g], 2 * (b % 2) + u, signal_words, b * ROW_WORDS + 2 * g * P + u, 2
                         )
             for g in range(PASSES):
                 copy = nc.scalar.copy if g % 2 == 0 else nc.vector.tensor_copy
@@ -100,8 +101,21 @@ def tile_graph_conv_pa_kernel(tc, signal, laplacian, x1_out, x2_out):
                 in_=x0_grouped[:, g * COLS * PACK : (g + 1) * COLS * PACK],
             )
 
-        def quantise_pair(r):
-            words = lap_pairs[r][:].bitcast(F32)
+        sorted_pairs = {}
+
+        def sort_words(r, e):
+            if e == 0:
+                sorted_pairs[r] = lap_sorted.tile([P, 2 * V], BF16, name="sorted_rows")
+            half = slice(e * ROW_WORDS, (e + 1) * ROW_WORDS)
+            nc.vector.tensor_copy(
+                out=sorted_pairs[r][:].bitcast(F32)[:, half].rearrange("p (g u i) -> p g u i", g=PASSES, u=2),
+                in_=lap_pairs[r][:].bitcast(F32)[:, half].rearrange("p (g i u) -> p g u i", g=PASSES, u=2),
+            )
+
+        def transpose_pair(r):
+            is_sorted = r in sorted_pairs
+            rows = sorted_pairs[r] if is_sorted else lap_pairs[r]
+            words = rows[:].bitcast(F32)
             grouped = lap_stage.tile([P, 2 * TILE_CODES * PACK], BF16, name="grouped", align_bytes=64)
             grouped_words = grouped[:].bitcast(F32).rearrange(
                 "p (n g i u) -> p n g i u", n=4, g=2, i=P, u=2
@@ -110,20 +124,26 @@ def tile_graph_conv_pa_kernel(tc, signal, laplacian, x1_out, x2_out):
             for n in range(4):
                 bank = new_bank()
                 for j in range(4):
-                    transpose_words(bank, j, words, (4 * n + 2 * (j // 2)) * P + j % 2)
+                    first = (4 * n + 2 * (j // 2)) * P
+                    if is_sorted:
+                        transpose_words(bank, j, words, first + (j % 2) * P, 1)
+                    else:
+                        transpose_words(bank, j, words, first + j % 2, 2)
                 banks.append(bank)
             for n in range(4):
                 nc.scalar.copy(
                     out=grouped_words[:, n],
                     in_=banks[n][:].rearrange("p (g u i) -> p g i u", g=2, u=2),
                 )
-            for e in range(2):
-                m = 2 * r + e
-                nc.vector.quantize_mx(
-                    out=lap_codes[:, m * TILE_CODES : (m + 1) * TILE_CODES].bitcast(FP8X4),
-                    scales=lap_scales[:, m * TILE_CODES : (m + 1) * TILE_CODES],
-                    in_=grouped[:, e * TILE_CODES * PACK : (e + 1) * TILE_CODES * PACK],
-                )
+            return grouped
+
+        def quantise_tile(r, e, grouped):
+            m = 2 * r + e
+            nc.vector.quantize_mx(
+                out=lap_codes[:, m * TILE_CODES : (m + 1) * TILE_CODES].bitcast(FP8X4),
+                scales=lap_scales[:, m * TILE_CODES : (m + 1) * TILE_CODES],
+                in_=grouped[:, e * TILE_CODES * PACK : (e + 1) * TILE_CODES * PACK],
+            )
 
         def multiply(acc, m, g, x_codes, x_scales):
             rows = slice((m * PASSES + g) * P, (m * PASSES + g + 1) * P)
@@ -142,28 +162,53 @@ def tile_graph_conv_pa_kernel(tc, signal, laplacian, x1_out, x2_out):
             g_rows, u_rows = divmod(r, 2)
             return pass_rows(out, g_rows)[:, 2 * u_rows : 2 * u_rows + 2, :]
 
-        quantise_pair(0)
-        x1_rows = None
+        x1_groups = {}
+
+        def group_x1(g):
+            x1_rows, x1_grouped = x1_groups[g]
+            nc.vector.tensor_copy(out=x1_grouped[:], in_=x1_rows[:].rearrange("p t c -> p c t"))
+
+        def quantise_x1(g):
+            nc.vector.quantize_mx(
+                out=x1_codes[:, g * COLS : (g + 1) * COLS].bitcast(FP8X4),
+                scales=x1_scales[:, g * COLS : (g + 1) * COLS],
+                in_=x1_groups[g][1][:].rearrange("p c t -> p (c t)"),
+            )
+
+        grouped = transpose_pair(0)
+        sort_words(1, 0)
+        quantise_tile(0, 0, grouped)
+        sort_words(1, 1)
+        quantise_tile(0, 1, grouped)
         for r in range(PAIRS):
-            if r + 1 < PAIRS:
-                quantise_pair(r + 1)
             g_out, u_out = divmod(r, 2)
+            g_done = g_out - 1 if u_out == 0 and g_out > 0 else None
+            if r + 1 < PAIRS:
+                grouped = transpose_pair(r + 1)
+                if r + 2 < PAIRS:
+                    sort_words(r + 2, 0)
+                if g_done is not None:
+                    group_x1(g_done)
+                quantise_tile(r + 1, 0, grouped)
+                if g_done is not None:
+                    quantise_x1(g_done)
+                if r + 2 < PAIRS:
+                    sort_words(r + 2, 1)
+                quantise_tile(r + 1, 1, grouped)
             if u_out == 0:
-                x1_rows = x1_stage.tile([P, PACK, COLS], F32, name="x1_rows")
+                x1_groups[g_out] = (
+                    x1_stage.tile([P, PACK, COLS], F32, name="x1_rows"),
+                    x1_stage.tile([P, COLS, PACK], BF16, name="x1_grouped", align_bytes=64),
+                )
+            x1_rows = x1_groups[g_out][0]
             for e in range(2):
                 acc = new_bank()
                 for g in range(PASSES):
                     multiply(acc, 2 * r + e, g, x0_codes, x0_scales)
                 nc.scalar.copy(out=x1_rows[:, 2 * u_out + e, :], in_=acc[:])
             nc.sync.dma_start(out=pair_of_rows(x1_out, r), in_=x1_rows[:, 2 * u_out : 2 * u_out + 2, :])
-            if u_out == 1:
-                x1_grouped = x1_stage.tile([P, COLS, PACK], BF16, name="x1_grouped", align_bytes=64)
-                nc.vector.tensor_copy(out=x1_grouped[:], in_=x1_rows[:].rearrange("p t c -> p c t"))
-                nc.vector.quantize_mx(
-                    out=x1_codes[:, g_out * COLS : (g_out + 1) * COLS].bitcast(FP8X4),
-                    scales=x1_scales[:, g_out * COLS : (g_out + 1) * COLS],
-                    in_=x1_grouped[:].rearrange("p c t -> p (c t)"),
-                )
+        group_x1(PASSES - 1)
+        quantise_x1(PASSES - 1)
 
         x0_values = x0_grouped[:].rearrange("p (g c t) -> p g c t", g=PASSES, c=COLS, t=PACK)
         x2_rows_of_pair = {}

@@ -50,17 +50,31 @@ def tile_graph_conv_pa_kernel(tc, signal, laplacian, x1_out, x2_out):
         lap_codes = keep.tile([P, ROW_TILES * TILE_CODES], U32, align_bytes=64)
         lap_scales = keep.tile([P, ROW_TILES * TILE_CODES], U8, align_bytes=64)
 
-        for b in range(BATCH):
-            nc.sync.dma_start(out=signal_rows[:, b * V : (b + 1) * V], in_=signal[b, :, :])
         lap_pairs = []
         for r in range(PAIRS):
-            pair_rows = lap_rows.tile([P, 2 * V], BF16, name="pair_rows")
+            lap_pairs.append(lap_rows.tile([P, 2 * V], BF16, name="pair_rows"))
+
+        def load_laplacian(r, first_tile, tiles):
             g_rows, u_rows = divmod(r, 2)
+            t = 2 * u_rows + first_tile
             nc.sync.dma_start(
-                out=pair_rows[:].rearrange("p (e k) -> p e k", e=2),
-                in_=pass_rows(laplacian, g_rows)[:, 2 * u_rows : 2 * u_rows + 2, :],
+                out=lap_pairs[r][:].rearrange("p (e k) -> p e k", e=2)[:, first_tile : first_tile + tiles, :],
+                in_=pass_rows(laplacian, g_rows)[:, t : t + tiles, :],
             )
-            lap_pairs.append(pair_rows)
+
+        signal_by_batch = signal_rows[:].rearrange("p (b v) -> p b v", b=BATCH)
+        half = V // 2
+        load_laplacian(0, 0, 1)
+        for b in range(2):
+            nc.sync.dma_start(out=signal_by_batch[:, b, :], in_=signal[b, :, :])
+        for v0 in (0, half):
+            nc.sync.dma_start(
+                out=signal_by_batch[:, 2:4, v0 : v0 + half],
+                in_=signal[2:4, :, v0 : v0 + half].rearrange("b c v -> c b v"),
+            )
+        load_laplacian(0, 1, 1)
+        for r in range(1, PAIRS):
+            load_laplacian(r, 0, 2)
 
         make_identity(nc, identity[:])
 
@@ -74,33 +88,6 @@ def tile_graph_conv_pa_kernel(tc, signal, laplacian, x1_out, x2_out):
                 identity[:],
             )
 
-        signal_words = signal_rows[:].bitcast(F32)
-        x0_words = x0_grouped[:].bitcast(F32).rearrange(
-            "p (g c b u) -> p g c b u", g=PASSES, c=P, b=BATCH, u=2
-        )
-        for h in range(2):
-            banks = []
-            for g in range(PASSES):
-                banks.append(new_bank())
-            for b in (2 * h, 2 * h + 1):
-                for g in range(PASSES):
-                    for u in range(2):
-                        transpose_words(
-                            banks[g], 2 * (b % 2) + u, signal_words, b * ROW_WORDS + 2 * g * P + u, 2
-                        )
-            for g in range(PASSES):
-                copy = nc.scalar.copy if g % 2 == 0 else nc.vector.tensor_copy
-                copy(
-                    out=x0_words[:, g, :, 2 * h : 2 * h + 2, :],
-                    in_=banks[g][:].rearrange("p (b u c) -> p c b u", b=2, u=2),
-                )
-        for g in range(PASSES):
-            nc.vector.quantize_mx(
-                out=x0_codes[:, g * COLS : (g + 1) * COLS].bitcast(FP8X4),
-                scales=x0_scales[:, g * COLS : (g + 1) * COLS],
-                in_=x0_grouped[:, g * COLS * PACK : (g + 1) * COLS * PACK],
-            )
-
         sorted_pairs = {}
 
         def sort_words(r, e):
@@ -112,16 +99,20 @@ def tile_graph_conv_pa_kernel(tc, signal, laplacian, x1_out, x2_out):
                 in_=lap_pairs[r][:].bitcast(F32)[:, half].rearrange("p (g i u) -> p g u i", g=PASSES, u=2),
             )
 
-        def transpose_pair(r):
+        grouped_pairs = {}
+
+        def transpose_tile(r, e, copies):
+            if e == 0:
+                grouped_pairs[r] = lap_stage.tile(
+                    [P, 2 * TILE_CODES * PACK], BF16, name="grouped", align_bytes=64
+                )
             is_sorted = r in sorted_pairs
             rows = sorted_pairs[r] if is_sorted else lap_pairs[r]
             words = rows[:].bitcast(F32)
-            grouped = lap_stage.tile([P, 2 * TILE_CODES * PACK], BF16, name="grouped", align_bytes=64)
-            grouped_words = grouped[:].bitcast(F32).rearrange(
+            grouped_words = grouped_pairs[r][:].bitcast(F32).rearrange(
                 "p (n g i u) -> p n g i u", n=4, g=2, i=P, u=2
             )
-            banks = []
-            for n in range(4):
+            for n in (2 * e, 2 * e + 1):
                 bank = new_bank()
                 for j in range(4):
                     first = (4 * n + 2 * (j // 2)) * P
@@ -129,27 +120,63 @@ def tile_graph_conv_pa_kernel(tc, signal, laplacian, x1_out, x2_out):
                         transpose_words(bank, j, words, first + (j % 2) * P, 1)
                     else:
                         transpose_words(bank, j, words, first + j % 2, 2)
-                banks.append(bank)
-            for n in range(4):
-                nc.scalar.copy(
+                copies[n % 2](
                     out=grouped_words[:, n],
-                    in_=banks[n][:].rearrange("p (g u i) -> p g i u", g=2, u=2),
+                    in_=bank[:].rearrange("p (g u i) -> p g i u", g=2, u=2),
                 )
-            return grouped
 
-        def quantise_tile(r, e, grouped):
+        def quantise_tile(r, e):
             m = 2 * r + e
             nc.vector.quantize_mx(
                 out=lap_codes[:, m * TILE_CODES : (m + 1) * TILE_CODES].bitcast(FP8X4),
                 scales=lap_scales[:, m * TILE_CODES : (m + 1) * TILE_CODES],
-                in_=grouped[:, e * TILE_CODES * PACK : (e + 1) * TILE_CODES * PACK],
+                in_=grouped_pairs[r][:, e * TILE_CODES * PACK : (e + 1) * TILE_CODES * PACK],
             )
 
-        def multiply(acc, m, g, x_codes, x_scales):
+        signal_words = signal_rows[:].bitcast(F32)
+        x0_words = x0_grouped[:].bitcast(F32).rearrange(
+            "p (g c b u) -> p g c b u", g=PASSES, c=P, b=BATCH, u=2
+        )
+
+        def transpose_signal(h, passes):
+            banks = {}
+            for g in passes:
+                banks[g] = new_bank()
+            for b in (2 * h, 2 * h + 1):
+                for g in passes:
+                    for u in range(2):
+                        transpose_words(
+                            banks[g], 2 * (b % 2) + u, signal_words, b * ROW_WORDS + 2 * g * P + u, 2
+                        )
+            for g in passes:
+                copy = nc.scalar.copy if g % 2 == 0 else nc.vector.tensor_copy
+                copy(
+                    out=x0_words[:, g, :, 2 * h : 2 * h + 2, :],
+                    in_=banks[g][:].rearrange("p (b u c) -> p c b u", b=2, u=2),
+                )
+
+        def quantise_x0(g):
+            nc.vector.quantize_mx(
+                out=x0_codes[:, g * COLS : (g + 1) * COLS].bitcast(FP8X4),
+                scales=x0_scales[:, g * COLS : (g + 1) * COLS],
+                in_=x0_grouped[:, g * COLS * PACK : (g + 1) * COLS * PACK],
+            )
+
+        transpose_tile(0, 0, (nc.scalar.copy, nc.vector.tensor_copy))
+        transpose_signal(0, range(PASSES))
+        quantise_tile(0, 0)
+        for g in (0, 2):
+            transpose_signal(1, (g, g + 1))
+            quantise_x0(g)
+            quantise_x0(g + 1)
+        transpose_tile(0, 1, (nc.scalar.copy, nc.scalar.copy))
+        quantise_tile(0, 1)
+
+        def multiply(acc, m, g, x_codes, x_scales, out_cols=slice(0, COLS)):
             rows = slice((m * PASSES + g) * P, (m * PASSES + g + 1) * P)
-            cols = slice(g * COLS, (g + 1) * COLS)
+            cols = slice(g * COLS + out_cols.start, g * COLS + out_cols.stop)
             nc.tensor.matmul_mx(
-                out=acc[:],
+                out=acc[:, out_cols],
                 lhsT=lap_codes[:, rows].bitcast(FP8X4),
                 lhsT_scale=lap_scales[:, rows],
                 rhs=x_codes[:, cols].bitcast(FP8X4),
@@ -175,60 +202,68 @@ def tile_graph_conv_pa_kernel(tc, signal, laplacian, x1_out, x2_out):
                 in_=x1_groups[g][1][:].rearrange("p c t -> p (c t)"),
             )
 
-        grouped = transpose_pair(0)
-        sort_words(1, 0)
-        quantise_tile(0, 0, grouped)
-        sort_words(1, 1)
-        quantise_tile(0, 1, grouped)
-        for r in range(PAIRS):
+        def multiply_tile(r, e):
             g_out, u_out = divmod(r, 2)
-            g_done = g_out - 1 if u_out == 0 and g_out > 0 else None
-            if r + 1 < PAIRS:
-                grouped = transpose_pair(r + 1)
-                if r + 2 < PAIRS:
-                    sort_words(r + 2, 0)
-                if g_done is not None:
-                    group_x1(g_done)
-                quantise_tile(r + 1, 0, grouped)
-                if g_done is not None:
-                    quantise_x1(g_done)
-                if r + 2 < PAIRS:
-                    sort_words(r + 2, 1)
-                quantise_tile(r + 1, 1, grouped)
-            if u_out == 0:
+            if u_out == 0 and e == 0:
                 x1_groups[g_out] = (
                     x1_stage.tile([P, PACK, COLS], F32, name="x1_rows"),
                     x1_stage.tile([P, COLS, PACK], BF16, name="x1_grouped", align_bytes=64),
                 )
             x1_rows = x1_groups[g_out][0]
-            for e in range(2):
-                acc = new_bank()
-                for g in range(PASSES):
-                    multiply(acc, 2 * r + e, g, x0_codes, x0_scales)
-                nc.scalar.copy(out=x1_rows[:, 2 * u_out + e, :], in_=acc[:])
-            nc.sync.dma_start(out=pair_of_rows(x1_out, r), in_=x1_rows[:, 2 * u_out : 2 * u_out + 2, :])
+            acc = new_bank()
+            for g in range(PASSES):
+                multiply(acc, 2 * r + e, g, x0_codes, x0_scales)
+            nc.scalar.copy(out=x1_rows[:, 2 * u_out + e, :], in_=acc[:])
+            if e == 1:
+                nc.sync.dma_start(
+                    out=pair_of_rows(x1_out, r), in_=x1_rows[:, 2 * u_out : 2 * u_out + 2, :]
+                )
+
+        multiply_tile(0, 0)
+        for r in range(PAIRS):
+            g_out, u_out = divmod(r, 2)
+            g_done = g_out - 1 if u_out == 0 and g_out > 0 else None
+            if r + 1 < PAIRS:
+                for e in range(2):
+                    transpose_tile(r + 1, e, (nc.scalar.copy, nc.scalar.copy))
+                if r + 2 < PAIRS:
+                    sort_words(r + 2, 0)
+                if g_done is not None:
+                    group_x1(g_done)
+                quantise_tile(r + 1, 0)
+                if g_done is not None:
+                    quantise_x1(g_done)
+                if r + 2 < PAIRS:
+                    sort_words(r + 2, 1)
+                quantise_tile(r + 1, 1)
+            if r > 0:
+                multiply_tile(r, 0)
+            multiply_tile(r, 1)
         group_x1(PASSES - 1)
         quantise_x1(PASSES - 1)
 
         x0_values = x0_grouped[:].rearrange("p (g c t) -> p g c t", g=PASSES, c=COLS, t=PACK)
         x2_rows_of_pair = {}
 
-        def finish_x2(acc, m):
+        def finish_x2(acc, m, cols, store_tiles):
             r, e = divmod(m, 2)
             g_out, u_out = divmod(r, 2)
-            if e == 0:
+            if r not in x2_rows_of_pair:
                 x2_rows_of_pair[r] = x2_stage.tile([P, 2, COLS], F32, name="x2_rows")
             x2_rows = x2_rows_of_pair[r]
             nc.vector.scalar_tensor_tensor(
-                out=x2_rows[:, e, :],
-                in0=acc[:],
+                out=x2_rows[:, e, cols],
+                in0=acc[:, cols],
                 scalar=2.0,
-                in1=x0_values[:, g_out, :, 2 * u_out + e],
+                in1=x0_values[:, g_out, cols, 2 * u_out + e],
                 op0=mybir.AluOpType.mult,
                 op1=mybir.AluOpType.subtract,
             )
-            if e == 1:
-                nc.sync.dma_start(out=pair_of_rows(x2_out, r), in_=x2_rows[:])
+            if store_tiles:
+                tiles = slice(e + 1 - store_tiles, e + 1)
+                nc.sync.dma_start(out=pair_of_rows(x2_out, r)[:, tiles, cols], in_=x2_rows[:, tiles, cols])
+
+        all_cols = slice(0, COLS)
 
         accs = []
         for m in range(PSUM_BANKS):
@@ -237,9 +272,15 @@ def tile_graph_conv_pa_kernel(tc, signal, laplacian, x1_out, x2_out):
             for m in range(PSUM_BANKS):
                 multiply(accs[m], m, g, x1_codes, x1_scales)
                 if g == PASSES - 1:
-                    finish_x2(accs[m], m)
+                    finish_x2(accs[m], m, all_cols, 2 if m % 2 else 0)
         for m in range(PSUM_BANKS, ROW_TILES):
-            acc = new_bank()
-            for g in range(PASSES):
-                multiply(acc, m, g, x1_codes, x1_scales)
-            finish_x2(acc, m)
+            if m < ROW_TILES - 1:
+                pieces = [all_cols]
+            else:
+                pieces = [slice(0, COLS // 2), slice(COLS // 2, COLS)]
+            for cols in pieces:
+                acc = new_bank()
+                for g in range(PASSES):
+                    multiply(acc, m, g, x1_codes, x1_scales, cols)
+                store_tiles = 1 if m >= ROW_TILES - 2 else 2 * (m % 2)
+                finish_x2(acc, m, cols, store_tiles)

@@ -62,16 +62,15 @@ def tile_graph_conv_pa_kernel(tc, signal, laplacian, x1_out, x2_out):
                 in_=pass_rows(laplacian, g_rows)[:, t : t + tiles, :],
             )
 
-        signal_by_batch = signal_rows[:].rearrange("p (b v) -> p b v", b=BATCH)
+        signal_by_half = signal_rows[:].rearrange("p (h b v) -> p h b v", h=2, b=BATCH)
         half = V // 2
         load_laplacian(0, 0, 1)
-        for b in range(2):
-            nc.sync.dma_start(out=signal_by_batch[:, b, :], in_=signal[b, :, :])
-        for v0 in (0, half):
-            nc.sync.dma_start(
-                out=signal_by_batch[:, 2:4, v0 : v0 + half],
-                in_=signal[2:4, :, v0 : v0 + half].rearrange("b c v -> c b v"),
-            )
+        for h in range(2):
+            for b in (0, 2):
+                nc.sync.dma_start(
+                    out=signal_by_half[:, h, b : b + 2, :],
+                    in_=signal[b : b + 2, :, h * half : (h + 1) * half].rearrange("b c v -> c b v"),
+                )
         load_laplacian(0, 1, 1)
         for r in range(1, PAIRS):
             load_laplacian(r, 0, 2)
@@ -145,9 +144,8 @@ def tile_graph_conv_pa_kernel(tc, signal, laplacian, x1_out, x2_out):
             for b in (2 * h, 2 * h + 1):
                 for g in passes:
                     for u in range(2):
-                        transpose_words(
-                            banks[g], 2 * (b % 2) + u, signal_words, b * ROW_WORDS + 2 * g * P + u, 2
-                        )
+                        first = ((g // 2) * BATCH + b) * (ROW_WORDS // 2) + (g % 2) * 2 * P + u
+                        transpose_words(banks[g], 2 * (b % 2) + u, signal_words, first, 2)
             for g in passes:
                 copy = nc.scalar.copy if g % 2 == 0 else nc.vector.tensor_copy
                 copy(
@@ -163,9 +161,9 @@ def tile_graph_conv_pa_kernel(tc, signal, laplacian, x1_out, x2_out):
             )
 
         transpose_tile(0, 0, (nc.scalar.copy, nc.vector.tensor_copy))
-        transpose_signal(0, range(PASSES))
         quantise_tile(0, 0)
         for g in (0, 2):
+            transpose_signal(0, (g, g + 1))
             transpose_signal(1, (g, g + 1))
             quantise_x0(g)
             quantise_x0(g + 1)
@@ -265,15 +263,16 @@ def tile_graph_conv_pa_kernel(tc, signal, laplacian, x1_out, x2_out):
 
         all_cols = slice(0, COLS)
 
+        early_tiles = 6
         accs = []
-        for m in range(PSUM_BANKS):
+        for m in range(early_tiles):
             accs.append(new_bank())
         for g in range(PASSES):
-            for m in range(PSUM_BANKS):
+            for m in range(early_tiles):
                 multiply(accs[m], m, g, x1_codes, x1_scales)
                 if g == PASSES - 1:
                     finish_x2(accs[m], m, all_cols, 2 if m % 2 else 0)
-        for m in range(PSUM_BANKS, ROW_TILES):
+        for m in range(early_tiles, ROW_TILES):
             if m < ROW_TILES - 1:
                 pieces = [all_cols]
             else:

@@ -33,8 +33,8 @@ def tile_graph_conv_pa_kernel(tc, signal, laplacian, x1_out, x2_out):
     with ExitStack() as ctx:
         keep = ctx.enter_context(tc.tile_pool(name="keep", bufs=1))
         lap_rows = ctx.enter_context(tc.tile_pool(name="lap_rows", bufs=PAIRS))
-        lap_sorted = ctx.enter_context(tc.tile_pool(name="lap_sorted", bufs=2))
-        lap_stage = ctx.enter_context(tc.tile_pool(name="lap_stage", bufs=2))
+        lap_sorted = ctx.enter_context(tc.tile_pool(name="lap_sorted", bufs=6))
+        lap_stage = ctx.enter_context(tc.tile_pool(name="lap_stage", bufs=4))
         x1_stage = ctx.enter_context(tc.tile_pool(name="x1_stage", bufs=2))
         x2_stage = ctx.enter_context(tc.tile_pool(name="x2_stage", bufs=3))
         psum = ctx.enter_context(tc.psum_pool(name="psum", bufs=PSUM_BANKS))
@@ -87,31 +87,27 @@ def tile_graph_conv_pa_kernel(tc, signal, laplacian, x1_out, x2_out):
                 identity[:],
             )
 
-        sorted_pairs = {}
+        sorted_tiles = {}
+        grouped_tiles = {}
 
-        def sort_words(r, e):
-            if e == 0:
-                sorted_pairs[r] = lap_sorted.tile([P, 2 * V], BF16, name="sorted_rows")
-            half = slice(e * ROW_WORDS, (e + 1) * ROW_WORDS)
+        def row_words(m):
+            return lap_pairs[m // 2][:].bitcast(F32)[:, m % 2 * ROW_WORDS : (m % 2 + 1) * ROW_WORDS]
+
+        def sort_tile(m):
+            sorted_tiles[m] = lap_sorted.tile([P, V], BF16, name="sorted_rows")
             nc.vector.tensor_copy(
-                out=sorted_pairs[r][:].bitcast(F32)[:, half].rearrange("p (g u i) -> p g u i", g=PASSES, u=2),
-                in_=lap_pairs[r][:].bitcast(F32)[:, half].rearrange("p (g i u) -> p g u i", g=PASSES, u=2),
+                out=sorted_tiles[m][:].bitcast(F32).rearrange("p (g u i) -> p g u i", g=PASSES, u=2),
+                in_=row_words(m).rearrange("p (g i u) -> p g u i", g=PASSES, u=2),
             )
 
-        grouped_pairs = {}
-
-        def transpose_tile(r, e, copies):
-            if e == 0:
-                grouped_pairs[r] = lap_stage.tile(
-                    [P, 2 * TILE_CODES * PACK], BF16, name="grouped", align_bytes=64
-                )
-            is_sorted = r in sorted_pairs
-            rows = sorted_pairs[r] if is_sorted else lap_pairs[r]
-            words = rows[:].bitcast(F32)
-            grouped_words = grouped_pairs[r][:].bitcast(F32).rearrange(
-                "p (n g i u) -> p n g i u", n=4, g=2, i=P, u=2
+        def transpose_tile(m, copies):
+            is_sorted = m in sorted_tiles
+            words = sorted_tiles[m][:].bitcast(F32) if is_sorted else row_words(m)
+            grouped_tiles[m] = lap_stage.tile([P, TILE_CODES * PACK], BF16, name="grouped", align_bytes=64)
+            grouped_words = grouped_tiles[m][:].bitcast(F32).rearrange(
+                "p (n g i u) -> p n g i u", n=2, g=2, i=P, u=2
             )
-            for n in (2 * e, 2 * e + 1):
+            for n in range(2):
                 bank = new_bank()
                 for j in range(4):
                     first = (4 * n + 2 * (j // 2)) * P
@@ -119,17 +115,16 @@ def tile_graph_conv_pa_kernel(tc, signal, laplacian, x1_out, x2_out):
                         transpose_words(bank, j, words, first + (j % 2) * P, 1)
                     else:
                         transpose_words(bank, j, words, first + j % 2, 2)
-                copies[n % 2](
+                copies[n](
                     out=grouped_words[:, n],
                     in_=bank[:].rearrange("p (g u i) -> p g i u", g=2, u=2),
                 )
 
-        def quantise_tile(r, e):
-            m = 2 * r + e
+        def quantise_tile(m):
             nc.vector.quantize_mx(
                 out=lap_codes[:, m * TILE_CODES : (m + 1) * TILE_CODES].bitcast(FP8X4),
                 scales=lap_scales[:, m * TILE_CODES : (m + 1) * TILE_CODES],
-                in_=grouped_pairs[r][:, e * TILE_CODES * PACK : (e + 1) * TILE_CODES * PACK],
+                in_=grouped_tiles[m][:],
             )
 
         signal_words = signal_rows[:].bitcast(F32)
@@ -160,15 +155,15 @@ def tile_graph_conv_pa_kernel(tc, signal, laplacian, x1_out, x2_out):
                 in_=x0_grouped[:, g * COLS * PACK : (g + 1) * COLS * PACK],
             )
 
-        transpose_tile(0, 0, (nc.scalar.copy, nc.vector.tensor_copy))
-        quantise_tile(0, 0)
+        transpose_tile(0, (nc.scalar.copy, nc.vector.tensor_copy))
+        quantise_tile(0)
         for g in (0, 2):
             transpose_signal(0, (g, g + 1))
             transpose_signal(1, (g, g + 1))
             quantise_x0(g)
             quantise_x0(g + 1)
-        transpose_tile(0, 1, (nc.scalar.copy, nc.scalar.copy))
-        quantise_tile(0, 1)
+        transpose_tile(1, (nc.scalar.copy, nc.scalar.copy))
+        quantise_tile(1)
 
         def multiply(acc, m, g, x_codes, x_scales, out_cols=slice(0, COLS)):
             rows = slice((m * PASSES + g) * P, (m * PASSES + g + 1) * P)
@@ -200,9 +195,9 @@ def tile_graph_conv_pa_kernel(tc, signal, laplacian, x1_out, x2_out):
                 in_=x1_groups[g][1][:].rearrange("p c t -> p (c t)"),
             )
 
-        def multiply_tile(r, e):
-            g_out, u_out = divmod(r, 2)
-            if u_out == 0 and e == 0:
+        def multiply_tile(m):
+            g_out, t = divmod(m, PACK)
+            if t == 0:
                 x1_groups[g_out] = (
                     x1_stage.tile([P, PACK, COLS], F32, name="x1_rows"),
                     x1_stage.tile([P, COLS, PACK], BF16, name="x1_grouped", align_bytes=64),
@@ -210,35 +205,42 @@ def tile_graph_conv_pa_kernel(tc, signal, laplacian, x1_out, x2_out):
             x1_rows = x1_groups[g_out][0]
             acc = new_bank()
             for g in range(PASSES):
-                multiply(acc, 2 * r + e, g, x0_codes, x0_scales)
-            nc.scalar.copy(out=x1_rows[:, 2 * u_out + e, :], in_=acc[:])
-            if e == 1:
-                nc.sync.dma_start(
-                    out=pair_of_rows(x1_out, r), in_=x1_rows[:, 2 * u_out : 2 * u_out + 2, :]
-                )
+                multiply(acc, m, g, x0_codes, x0_scales)
+            nc.scalar.copy(out=x1_rows[:, t, :], in_=acc[:])
+            if t % 2 == 1:
+                nc.sync.dma_start(out=pair_of_rows(x1_out, m // 2), in_=x1_rows[:, t - 1 : t + 1, :])
 
-        multiply_tile(0, 0)
-        for r in range(PAIRS):
-            g_out, u_out = divmod(r, 2)
-            g_done = g_out - 1 if u_out == 0 and g_out > 0 else None
-            if r + 1 < PAIRS:
-                for e in range(2):
-                    transpose_tile(r + 1, e, (nc.scalar.copy, nc.scalar.copy))
-                if r + 2 < PAIRS:
-                    sort_words(r + 2, 0)
-                if g_done is not None:
-                    group_x1(g_done)
-                quantise_tile(r + 1, 0)
-                if g_done is not None:
-                    quantise_x1(g_done)
-                if r + 2 < PAIRS:
-                    sort_words(r + 2, 1)
-                quantise_tile(r + 1, 1)
-            if r > 0:
-                multiply_tile(r, 0)
-            multiply_tile(r, 1)
-        group_x1(PASSES - 1)
-        quantise_x1(PASSES - 1)
+        runs = [(2, 3), (4, 5, 6), (7, 8, 9), (10, 11, 12), (13, 14, 15)]
+        multiply_tile(0)
+        ready = (1,)
+        rounded = 0
+        for i, run in enumerate(runs):
+            for m in run:
+                transpose_tile(m, (nc.scalar.copy, nc.scalar.copy))
+            x1_done = ready[0] // PACK
+            to_sort = list(runs[i + 1]) if i + 1 < len(runs) else []
+            for j in range(len(run)):
+                if to_sort:
+                    sort_tile(to_sort.pop(0))
+                if j == 0 and x1_done > rounded:
+                    group_x1(rounded)
+                quantise_tile(run[j])
+                if j == 0 and x1_done > rounded:
+                    quantise_x1(rounded)
+                    rounded += 1
+            for m in to_sort:
+                sort_tile(m)
+            for m in ready:
+                multiply_tile(m)
+            ready = run
+        for m in ready:
+            multiply_tile(m)
+            if m == ready[0]:
+                group_x1(rounded)
+                quantise_x1(rounded)
+                rounded += 1
+        group_x1(rounded)
+        quantise_x1(rounded)
 
         x0_values = x0_grouped[:].rearrange("p (g c t) -> p g c t", g=PASSES, c=COLS, t=PACK)
         x2_rows_of_pair = {}

@@ -20,6 +20,7 @@ PAIRS = ROW_TILES // 2
 ROW_WORDS = V // 2
 TILE_CODES = PASSES * P
 PSUM_BANKS = 8
+FIRST_SORTED = 5
 
 FLOPS = 2 * 2 * V * V * COLS
 
@@ -33,8 +34,9 @@ def tile_graph_conv_pa_kernel(tc, signal, laplacian, x1_out, x2_out):
     with ExitStack() as ctx:
         keep = ctx.enter_context(tc.tile_pool(name="keep", bufs=1))
         lap_rows = ctx.enter_context(tc.tile_pool(name="lap_rows", bufs=PAIRS))
-        lap_sorted = ctx.enter_context(tc.tile_pool(name="lap_sorted", bufs=6))
+        lap_sorted = ctx.enter_context(tc.tile_pool(name="lap_sorted", bufs=4))
         lap_stage = ctx.enter_context(tc.tile_pool(name="lap_stage", bufs=4))
+        x1_sums = ctx.enter_context(tc.tile_pool(name="x1_sums", bufs=3))
         x1_stage = ctx.enter_context(tc.tile_pool(name="x1_stage", bufs=2))
         x2_stage = ctx.enter_context(tc.tile_pool(name="x2_stage", bufs=3))
         psum = ctx.enter_context(tc.psum_pool(name="psum", bufs=PSUM_BANKS))
@@ -182,65 +184,58 @@ def tile_graph_conv_pa_kernel(tc, signal, laplacian, x1_out, x2_out):
             g_rows, u_rows = divmod(r, 2)
             return pass_rows(out, g_rows)[:, 2 * u_rows : 2 * u_rows + 2, :]
 
-        x1_groups = {}
+        x1_rows = {}
+        x1_grouped = {}
 
         def group_x1(g):
-            x1_rows, x1_grouped = x1_groups[g]
-            nc.vector.tensor_copy(out=x1_grouped[:], in_=x1_rows[:].rearrange("p t c -> p c t"))
+            x1_grouped[g] = x1_stage.tile([P, COLS, PACK], BF16, name="x1_grouped", align_bytes=64)
+            nc.vector.tensor_copy(out=x1_grouped[g][:], in_=x1_rows[g][:].rearrange("p t c -> p c t"))
 
         def quantise_x1(g):
             nc.vector.quantize_mx(
                 out=x1_codes[:, g * COLS : (g + 1) * COLS].bitcast(FP8X4),
                 scales=x1_scales[:, g * COLS : (g + 1) * COLS],
-                in_=x1_groups[g][1][:].rearrange("p c t -> p (c t)"),
+                in_=x1_grouped[g][:].rearrange("p c t -> p (c t)"),
             )
 
         def multiply_tile(m):
             g_out, t = divmod(m, PACK)
             if t == 0:
-                x1_groups[g_out] = (
-                    x1_stage.tile([P, PACK, COLS], F32, name="x1_rows"),
-                    x1_stage.tile([P, COLS, PACK], BF16, name="x1_grouped", align_bytes=64),
-                )
-            x1_rows = x1_groups[g_out][0]
+                x1_rows[g_out] = x1_sums.tile([P, PACK, COLS], F32, name="x1_rows")
             acc = new_bank()
             for g in range(PASSES):
                 multiply(acc, m, g, x0_codes, x0_scales)
-            nc.scalar.copy(out=x1_rows[:, t, :], in_=acc[:])
+            nc.scalar.copy(out=x1_rows[g_out][:, t, :], in_=acc[:])
             if t % 2 == 1:
-                nc.sync.dma_start(out=pair_of_rows(x1_out, m // 2), in_=x1_rows[:, t - 1 : t + 1, :])
+                nc.sync.dma_start(out=pair_of_rows(x1_out, m // 2), in_=x1_rows[g_out][:, t - 1 : t + 1, :])
 
         runs = [(2, 3), (4, 5, 6), (7, 8, 9), (10, 11, 12), (13, 14, 15)]
         multiply_tile(0)
         ready = (1,)
-        rounded = 0
         for i, run in enumerate(runs):
             for m in run:
                 transpose_tile(m, (nc.scalar.copy, nc.scalar.copy))
-            x1_done = ready[0] // PACK
-            to_sort = list(runs[i + 1]) if i + 1 < len(runs) else []
-            for j in range(len(run)):
-                if to_sort:
-                    sort_tile(to_sort.pop(0))
-                if j == 0 and x1_done > rounded:
-                    group_x1(rounded)
-                quantise_tile(run[j])
-                if j == 0 and x1_done > rounded:
-                    quantise_x1(rounded)
-                    rounded += 1
-            for m in to_sort:
-                sort_tile(m)
+            last = i + 1 == len(runs)
+            to_sort = [] if last else [m for m in runs[i + 1] if m >= FIRST_SORTED]
+            if last:
+                group_x1(0)
+            for j in range(max(len(run), len(to_sort))):
+                if j < len(to_sort):
+                    sort_tile(to_sort[j])
+                if j < len(run):
+                    quantise_tile(run[j])
+            if last:
+                quantise_x1(0)
+                group_x1(1)
+                quantise_x1(1)
             for m in ready:
                 multiply_tile(m)
             ready = run
         for m in ready:
             multiply_tile(m)
-            if m == ready[0]:
-                group_x1(rounded)
-                quantise_x1(rounded)
-                rounded += 1
-        group_x1(rounded)
-        quantise_x1(rounded)
+        for g in (2, 3):
+            group_x1(g)
+            quantise_x1(g)
 
         x0_values = x0_grouped[:].rearrange("p (g c t) -> p g c t", g=PASSES, c=COLS, t=PACK)
         x2_rows_of_pair = {}
@@ -265,7 +260,7 @@ def tile_graph_conv_pa_kernel(tc, signal, laplacian, x1_out, x2_out):
 
         all_cols = slice(0, COLS)
 
-        early_tiles = 6
+        early_tiles = 7
         accs = []
         for m in range(early_tiles):
             accs.append(new_bank())

from contextlib import ExitStack

import concourse.mybir as mybir
from concourse.masks import make_identity

F32 = mybir.dt.float32
BF16 = mybir.dt.bfloat16
U32 = mybir.dt.uint32
U8 = mybir.dt.uint8
FP8X4 = mybir.dt.float8_e4m3fn_x4

P = 128
PACK = 4
V = 2048
BATCH = 4
COLS = 512
PASSES = V // (P * PACK)
ROW_TILES = V // P
PAIRS = ROW_TILES // 2
ROW_WORDS = V // 2
TILE_CODES = PASSES * P
PSUM_BANKS = 8
FIRST_SORTED = 5

FLOPS = 2 * 2 * V * V * COLS


def pass_rows(matrix, g):
    return matrix[PACK * P * g : PACK * P * (g + 1), :].rearrange("(p t) c -> p t c", t=PACK)


def tile_graph_conv_pa_kernel(tc, signal, laplacian, x1_out, x2_out):
    nc = tc.nc
    with ExitStack() as ctx:
        keep = ctx.enter_context(tc.tile_pool(name="keep", bufs=1))
        lap_rows = ctx.enter_context(tc.tile_pool(name="lap_rows", bufs=PAIRS))
        lap_sorted = ctx.enter_context(tc.tile_pool(name="lap_sorted", bufs=4))
        lap_stage = ctx.enter_context(tc.tile_pool(name="lap_stage", bufs=4))
        x1_sums = ctx.enter_context(tc.tile_pool(name="x1_sums", bufs=3))
        x1_stage = ctx.enter_context(tc.tile_pool(name="x1_stage", bufs=2))
        x2_stage = ctx.enter_context(tc.tile_pool(name="x2_stage", bufs=3))
        psum = ctx.enter_context(tc.psum_pool(name="psum", bufs=PSUM_BANKS))
        ctx.enter_context(tc.manual_schedule())

        identity = keep.tile([P, P], F32)
        signal_rows = keep.tile([P, BATCH * V], BF16)
        x0_grouped = keep.tile([P, PASSES * COLS * PACK], BF16, align_bytes=64)
        x0_codes = keep.tile([P, PASSES * COLS], U32, align_bytes=64)
        x0_scales = keep.tile([P, PASSES * COLS], U8, align_bytes=64)
        x1_codes = keep.tile([P, PASSES * COLS], U32, align_bytes=64)
        x1_scales = keep.tile([P, PASSES * COLS], U8, align_bytes=64)
        lap_codes = keep.tile([P, ROW_TILES * TILE_CODES], U32, align_bytes=64)
        lap_scales = keep.tile([P, ROW_TILES * TILE_CODES], U8, align_bytes=64)

        lap_pairs = []
        for r in range(PAIRS):
            lap_pairs.append(lap_rows.tile([P, 2 * V], BF16, name="pair_rows"))

        def load_laplacian(r, first_tile, tiles):
            g_rows, u_rows = divmod(r, 2)
            t = 2 * u_rows + first_tile
            nc.sync.dma_start(
                out=lap_pairs[r][:].rearrange("p (e k) -> p e k", e=2)[:, first_tile : first_tile + tiles, :],
                in_=pass_rows(laplacian, g_rows)[:, t : t + tiles, :],
            )

        signal_by_half = signal_rows[:].rearrange("p (h b v) -> p h b v", h=2, b=BATCH)
        half = V // 2
        load_laplacian(0, 0, 1)
        for h in range(2):
            for b in (0, 2):
                nc.sync.dma_start(
                    out=signal_by_half[:, h, b : b + 2, :],
                    in_=signal[b : b + 2, :, h * half : (h + 1) * half].rearrange("b c v -> c b v"),
                )
        load_laplacian(0, 1, 1)
        for r in range(1, PAIRS):
            load_laplacian(r, 0, 2)

        make_identity(nc, identity[:])

        def new_bank():
            return psum.tile([P, COLS], F32, name="bank")

        def transpose_words(bank, j, words, first_word, step):
            nc.tensor.transpose(
                bank[:, j * P : (j + 1) * P],
                words[:, first_word : first_word + step * (P - 1) + 1 : step],
                identity[:],
            )

        sorted_tiles = {}
        grouped_tiles = {}

        def row_words(m):
            return lap_pairs[m // 2][:].bitcast(F32)[:, m % 2 * ROW_WORDS : (m % 2 + 1) * ROW_WORDS]

        def sort_tile(m):
            sorted_tiles[m] = lap_sorted.tile([P, V], BF16, name="sorted_rows")
            nc.vector.tensor_copy(
                out=sorted_tiles[m][:].bitcast(F32).rearrange("p (g u i) -> p g u i", g=PASSES, u=2),
                in_=row_words(m).rearrange("p (g i u) -> p g u i", g=PASSES, u=2),
            )

        def transpose_tile(m, copies):
            is_sorted = m in sorted_tiles
            words = sorted_tiles[m][:].bitcast(F32) if is_sorted else row_words(m)
            grouped_tiles[m] = lap_stage.tile([P, TILE_CODES * PACK], BF16, name="grouped", align_bytes=64)
            grouped_words = grouped_tiles[m][:].bitcast(F32).rearrange(
                "p (n g i u) -> p n g i u", n=2, g=2, i=P, u=2
            )
            for n in range(2):
                bank = new_bank()
                for j in range(4):
                    first = (4 * n + 2 * (j // 2)) * P
                    if is_sorted:
                        transpose_words(bank, j, words, first + (j % 2) * P, 1)
                    else:
                        transpose_words(bank, j, words, first + j % 2, 2)
                copies[n](
                    out=grouped_words[:, n],
                    in_=bank[:].rearrange("p (g u i) -> p g i u", g=2, u=2),
                )

        def quantise_tile(m):
            nc.vector.quantize_mx(
                out=lap_codes[:, m * TILE_CODES : (m + 1) * TILE_CODES].bitcast(FP8X4),
                scales=lap_scales[:, m * TILE_CODES : (m + 1) * TILE_CODES],
                in_=grouped_tiles[m][:],
            )

        signal_words = signal_rows[:].bitcast(F32)
        x0_words = x0_grouped[:].bitcast(F32).rearrange(
            "p (g c b u) -> p g c b u", g=PASSES, c=P, b=BATCH, u=2
        )

        def transpose_signal(h, passes):
            banks = {}
            for g in passes:
                banks[g] = new_bank()
            for b in (2 * h, 2 * h + 1):
                for g in passes:
                    for u in range(2):
                        first = ((g // 2) * BATCH + b) * (ROW_WORDS // 2) + (g % 2) * 2 * P + u
                        transpose_words(banks[g], 2 * (b % 2) + u, signal_words, first, 2)
            for g in passes:
                copy = nc.scalar.copy if g % 2 == 0 else nc.vector.tensor_copy
                copy(
                    out=x0_words[:, g, :, 2 * h : 2 * h + 2, :],
                    in_=banks[g][:].rearrange("p (b u c) -> p c b u", b=2, u=2),
                )

        def quantise_x0(g):
            nc.vector.quantize_mx(
                out=x0_codes[:, g * COLS : (g + 1) * COLS].bitcast(FP8X4),
                scales=x0_scales[:, g * COLS : (g + 1) * COLS],
                in_=x0_grouped[:, g * COLS * PACK : (g + 1) * COLS * PACK],
            )

        transpose_tile(0, (nc.scalar.copy, nc.vector.tensor_copy))
        quantise_tile(0)
        for g in (0, 2):
            transpose_signal(0, (g, g + 1))
            transpose_signal(1, (g, g + 1))
            quantise_x0(g)
            quantise_x0(g + 1)
        transpose_tile(1, (nc.scalar.copy, nc.scalar.copy))
        quantise_tile(1)

        def multiply(acc, m, g, x_codes, x_scales, out_cols=slice(0, COLS)):
            rows = slice((m * PASSES + g) * P, (m * PASSES + g + 1) * P)
            cols = slice(g * COLS + out_cols.start, g * COLS + out_cols.stop)
            nc.tensor.matmul_mx(
                out=acc[:, out_cols],
                lhsT=lap_codes[:, rows].bitcast(FP8X4),
                lhsT_scale=lap_scales[:, rows],
                rhs=x_codes[:, cols].bitcast(FP8X4),
                rhs_scale=x_scales[:, cols],
                start=(g == 0),
                stop=(g == PASSES - 1),
            )

        def pair_of_rows(out, r):
            g_rows, u_rows = divmod(r, 2)
            return pass_rows(out, g_rows)[:, 2 * u_rows : 2 * u_rows + 2, :]

        x1_rows = {}
        x1_grouped = {}

        def group_x1(g):
            x1_grouped[g] = x1_stage.tile([P, COLS, PACK], BF16, name="x1_grouped", align_bytes=64)
            nc.vector.tensor_copy(out=x1_grouped[g][:], in_=x1_rows[g][:].rearrange("p t c -> p c t"))

        def quantise_x1(g):
            nc.vector.quantize_mx(
                out=x1_codes[:, g * COLS : (g + 1) * COLS].bitcast(FP8X4),
                scales=x1_scales[:, g * COLS : (g + 1) * COLS],
                in_=x1_grouped[g][:].rearrange("p c t -> p (c t)"),
            )

        def multiply_tile(m):
            g_out, t = divmod(m, PACK)
            if t == 0:
                x1_rows[g_out] = x1_sums.tile([P, PACK, COLS], F32, name="x1_rows")
            acc = new_bank()
            for g in range(PASSES):
                multiply(acc, m, g, x0_codes, x0_scales)
            nc.scalar.copy(out=x1_rows[g_out][:, t, :], in_=acc[:])
            if t % 2 == 1:
                nc.sync.dma_start(out=pair_of_rows(x1_out, m // 2), in_=x1_rows[g_out][:, t - 1 : t + 1, :])

        runs = [(2, 3), (4, 5, 6), (7, 8, 9), (10, 11, 12), (13, 14, 15)]
        multiply_tile(0)
        ready = (1,)
        for i, run in enumerate(runs):
            for m in run:
                transpose_tile(m, (nc.scalar.copy, nc.scalar.copy))
            last = i + 1 == len(runs)
            to_sort = [] if last else [m for m in runs[i + 1] if m >= FIRST_SORTED]
            if last:
                group_x1(0)
            for j in range(max(len(run), len(to_sort))):
                if j < len(to_sort):
                    sort_tile(to_sort[j])
                if j < len(run):
                    quantise_tile(run[j])
            if last:
                quantise_x1(0)
                group_x1(1)
                quantise_x1(1)
            for m in ready:
                multiply_tile(m)
            ready = run
        for m in ready:
            multiply_tile(m)
        for g in (2, 3):
            group_x1(g)
            quantise_x1(g)

        x0_values = x0_grouped[:].rearrange("p (g c t) -> p g c t", g=PASSES, c=COLS, t=PACK)
        x2_rows_of_pair = {}

        def finish_x2(acc, m, cols, store_tiles):
            r, e = divmod(m, 2)
            g_out, u_out = divmod(r, 2)
            if r not in x2_rows_of_pair:
                x2_rows_of_pair[r] = x2_stage.tile([P, 2, COLS], F32, name="x2_rows")
            x2_rows = x2_rows_of_pair[r]
            nc.vector.scalar_tensor_tensor(
                out=x2_rows[:, e, cols],
                in0=acc[:, cols],
                scalar=2.0,
                in1=x0_values[:, g_out, cols, 2 * u_out + e],
                op0=mybir.AluOpType.mult,
                op1=mybir.AluOpType.subtract,
            )
            if store_tiles:
                tiles = slice(e + 1 - store_tiles, e + 1)
                nc.sync.dma_start(out=pair_of_rows(x2_out, r)[:, tiles, cols], in_=x2_rows[:, tiles, cols])

        all_cols = slice(0, COLS)

        early_tiles = 7
        accs = []
        for m in range(early_tiles):
            accs.append(new_bank())
        for g in range(PASSES):
            for m in range(early_tiles):
                multiply(accs[m], m, g, x1_codes, x1_scales)
                if g == PASSES - 1:
                    finish_x2(accs[m], m, all_cols, 2 if m % 2 else 0)
        for m in range(early_tiles, ROW_TILES):
            if m < ROW_TILES - 1:
                pieces = [all_cols]
            else:
                pieces = [slice(0, COLS // 2), slice(COLS // 2, COLS)]
            for cols in pieces:
                acc = new_bank()
                for g in range(PASSES):
                    multiply(acc, m, g, x1_codes, x1_scales, cols)
                store_tiles = 1 if m >= ROW_TILES - 2 else 2 * (m % 2)
                finish_x2(acc, m, cols, store_tiles)
